import numpy as np
import ml_dtypes


def mxq(x, axis, fmt="e4m3"):
    dtype, down = {"e4m3": (ml_dtypes.float8_e4m3fn, 7), "e5m2": (ml_dtypes.float8_e5m2, 14)}[fmt]
    v = np.moveaxis(np.asarray(x, np.float32).astype(ml_dtypes.bfloat16).astype(np.float64), axis, -1)
    blocks = v.reshape(v.shape[:-1] + (-1, 32))
    amax = np.abs(blocks).max(-1, keepdims=True)
    byte = np.maximum(np.where(amax > 0, np.frexp(amax)[1] - 1 + 127, 0) - down, 1)
    scale = np.exp2(byte - 127.0)
    codes = (blocks / scale).astype(np.float32).astype(dtype).astype(np.float64)
    return np.moveaxis((codes * scale).reshape(v.shape), -1, axis)


WIDE = False


def mx_kscale(k):
    if not WIDE:
        return np.ones(k)
    levels = np.array([10, -10, 5, -5, 0])
    a = np.random.permutation(np.resize(levels, k // 512 * 4)).reshape(k // 512, 4)
    idx = np.arange(k)
    return np.exp2(a[idx // 512, idx % 128 // 32])


BF16 = ml_dtypes.bfloat16


def bf(x):
    return np.asarray(x, np.float32).astype(BF16)


def f64(x):
    return np.asarray(x).astype(np.float64)


B, S, D, H, QK = 8, 1024, 1024, 64, 128
EPS = 1e-5
R = np.sqrt(0.1 * S / np.sqrt(QK))


def silu(a):
    return a / (1.0 + np.exp(-a))


def setup_inputs():
    s = mx_kscale(D)
    return {
        "x": bf(np.random.standard_normal((B, S, D)) + 0.5 * np.random.standard_normal((B, S, 1))),
        "ln_w": bf((1.0 + 0.1 * np.random.standard_normal(D)) * s),
        "ln_b": bf(0.1 * np.random.standard_normal(D) * s),
        "W_hidden": bf(np.random.standard_normal((2 * H, D)) / np.sqrt(D) / s),
        "b_hidden": bf(0.1 * np.random.standard_normal(2 * H)),
        "W_qk": bf(np.random.standard_normal((QK, D)) / np.sqrt(D) / s),
        "b_qk": bf(0.1 * np.random.standard_normal(QK)),
        "gamma": bf(np.random.standard_normal((2, QK)) * R / 0.6),
        "beta": bf(np.random.standard_normal((2, QK)) * R * 0.3),
    }


def reference(x, ln_w, ln_b, W_hidden, b_hidden, W_qk, b_qk, gamma, beta):
    x = f64(x)
    mu = x.mean(-1, keepdims=True)
    var = np.square(x - mu).mean(-1, keepdims=True)
    normed = (x - mu) / np.sqrt(var + EPS) * f64(ln_w) + f64(ln_b)
    nq = mxq(normed, 2, "e4m3")
    hg = silu((nq @ mxq(f64(W_hidden), 1, "e4m3").T) + f64(b_hidden))
    v, gate = hg[..., :H], hg[..., H:]
    Z = silu((nq @ mxq(f64(W_qk), 1, "e4m3").T) + f64(b_qk))
    gamma, beta = f64(gamma), f64(beta)
    q = Z * gamma[0] + beta[0]
    k = Z * gamma[1] + beta[1]
    return v, gate, q, k

@@ -1,0 +1,214 @@
+from contextlib import ExitStack
+
+import concourse.mybir as mybir
+from concourse.masks import make_identity
+
+F32 = mybir.dt.float32
+BF16 = mybir.dt.bfloat16
+U32 = mybir.dt.uint32
+U8 = mybir.dt.uint8
+FP8X4 = mybir.dt.float8_e4m3fn_x4
+ALU = mybir.AluOpType
+ACT = mybir.ActivationFunctionType
+
+P = 128
+D = 1024
+ROWS = 8192
+JT = 4
+SUP = P * JT
+NSUP = ROWS // SUP
+KB = D // P
+EPS = 1e-5
+FLOPS = 2 * ROWS * D * 256
+
+B_ENGINE = ("g", "g", "g", "s")
+EVAC_ENGINE = ("s", "s", "s")
+
+
+def tile_gau_pb_t_kernel(
+    tc, x, ln_w, ln_b, W_hidden, b_hidden, W_qk, b_qk, gamma, beta, out_0, out_1, out_2, out_3
+):
+    nc = tc.nc
+    xf = x.flatten_outer_dims()
+    vf = out_0.flatten_outer_dims()
+    gf = out_1.flatten_outer_dims()
+    qf = out_2.flatten_outer_dims()
+    kf = out_3.flatten_outer_dims()
+
+    with ExitStack() as ctx:
+        keep = ctx.enter_context(tc.tile_pool(name="keep", bufs=1))
+        xpool = ctx.enter_context(tc.tile_pool(name="xpool", bufs=4))
+        small = ctx.enter_context(tc.tile_pool(name="small", bufs=4))
+        ypool = ctx.enter_context(tc.tile_pool(name="ypool", bufs=2))
+        upool = ctx.enter_context(tc.tile_pool(name="upool", bufs=2))
+        gpool = ctx.enter_context(tc.tile_pool(name="gpool", bufs=2))
+        cpool = ctx.enter_context(tc.tile_pool(name="cpool", bufs=2))
+        epool = ctx.enter_context(tc.tile_pool(name="epool", bufs=2))
+        opool = ctx.enter_context(tc.tile_pool(name="opool", bufs=2))
+        ps_in = ctx.enter_context(tc.psum_pool(name="ps_in", bufs=4))
+        ps_acc = ctx.enter_context(tc.psum_pool(name="ps_acc", bufs=1))
+        ps_out = ctx.enter_context(tc.psum_pool(name="ps_out", bufs=2))
+
+        ident = keep.tile([P, P], F32, name="ident")
+        make_identity(nc, ident[:])
+        mhalf = keep.tile([P, JT], F32, name="mhalf")
+        nc.vector.memset(mhalf[:], -0.5)
+
+        cst_b = keep.tile([P, P], BF16, name="cst_b")
+        nc.vector.memset(cst_b[:], 0.0)
+        nc.scalar.dma_start(out=cst_b[0:8, :], in_=ln_w.rearrange("(a b) -> a b", b=P))
+        nc.scalar.dma_start(out=cst_b[8:16, :], in_=ln_b.rearrange("(a b) -> a b", b=P))
+        nc.scalar.dma_start(out=cst_b[16:17, :], in_=b_hidden.rearrange("(a b) -> a b", b=P))
+        nc.scalar.dma_start(out=cst_b[17:18, :], in_=b_qk.rearrange("(a b) -> a b", b=P))
+        nc.scalar.dma_start(out=cst_b[18:20, :], in_=gamma)
+        nc.scalar.dma_start(out=cst_b[20:22, :], in_=beta)
+        cst_f = keep.tile([P, P], F32, name="cst_f")
+        nc.vector.tensor_copy(out=cst_f[:], in_=cst_b[:])
+        tpc = ps_in.tile([P, 512], F32, tag="tin", name="tpc")
+        nc.tensor.transpose(tpc[:, 0:P], cst_f[:], ident[:])
+        cols = keep.tile([P, 32], F32, name="cols")
+        nc.vector.tensor_copy(out=cols[:, 0:22], in_=tpc[:, 0:22])
+
+        wgrp = keep.tile([P, 4, P, 4], BF16, name="wgrp", align_bytes=64)
+        wcodes = keep.tile([P, 4, P], U32, name="wcodes", align_bytes=64)
+        wsc = keep.tile([P, 4, P], U8, name="wsc", align_bytes=64)
+        for h, W in enumerate((W_hidden, W_qk)):
+            wb = keep.tile([P, D], BF16, name="wb%d" % h)
+            nc.scalar.dma_start(out=wb[:], in_=W)
+            wf = keep.tile([P, D], F32, name="wf%d" % h)
+            nc.vector.tensor_copy(out=wf[:], in_=wb[:])
+            for g in range(2):
+                tpw = ps_in.tile([P, 512], F32, tag="tin", name="tpw")
+                for t in range(4):
+                    c0 = 512 * g + P * t
+                    nc.tensor.transpose(tpw[:, P * t : P * (t + 1)], wf[:, c0 : c0 + P], ident[:])
+                nc.vector.tensor_copy(
+                    out=wgrp[:, 2 * h + g, :, :], in_=tpw[:].rearrange("p (t o) -> p o t", t=4)
+                )
+        nc.vector.quantize_mx(
+            out=wcodes[:].rearrange("p a o -> p (a o)").bitcast(FP8X4),
+            scales=wsc[:].rearrange("p a o -> p (a o)"),
+            in_=wgrp[:].rearrange("p a o t -> p (a o t)"),
+        )
+
+        for s in range(NSUP):
+            r0 = SUP * s
+            xs = xpool.tile([P, JT, D], BF16, name="xs")
+            nc.sync.dma_start(out=xs[:], in_=xf[r0 : r0 + SUP, :].rearrange("(p j) k -> p j k", j=JT))
+
+            st = small.tile([P, JT, 2, 6], F32, name="st")
+            mv = small.tile([P, JT, 2], F32, name="mv")
+            for j in range(JT):
+                for c in range(2):
+                    nc.vector.bn_stats(out=st[:, j, c, :], in_=xs[:, j, 512 * c : 512 * (c + 1)])
+                nc.vector.bn_aggr(out=mv[:, j, :], in_=st[:, j, :, :].rearrange("p c v -> p (c v)"))
+            ve = small.tile([P, JT], F32, name="ve")
+            nc.vector.tensor_scalar_add(out=ve[:], in0=mv[:, :, 1], scalar1=EPS)
+            negmu = small.tile([P, JT], F32, name="negmu")
+            nc.vector.tensor_scalar_mul(out=negmu[:], in0=mv[:, :, 0], scalar1=-1.0)
+            rstd = small.tile([P, JT], F32, name="rstd")
+            nc.gpsimd.tensor_tensor(out=rstd[:], in0=ve[:], in1=mhalf[:], op=ALU.pow)
+            nmr = small.tile([P, JT], F32, name="nmr")
+            nc.vector.tensor_mul(out=nmr[:], in0=negmu[:], in1=rstd[:])
+
+            y = ypool.tile([P, JT, D], F32, name="y")
+            for j in range(JT):
+                if B_ENGINE[j] == "g":
+                    nc.gpsimd.tensor_scalar(
+                        out=y[:, j, :], in0=xs[:, j, :],
+                        scalar1=negmu[:, j : j + 1], scalar2=rstd[:, j : j + 1],
+                        op0=ALU.add, op1=ALU.mult,
+                    )
+                elif B_ENGINE[j] == "s":
+                    nc.scalar.activation(
+                        out=y[:, j, :], in_=xs[:, j, :], func=ACT.Identity,
+                        bias=nmr[:, j : j + 1], scale=rstd[:, j : j + 1],
+                    )
+                else:
+                    nc.vector.tensor_scalar(
+                        out=y[:, j, :], in0=xs[:, j, :],
+                        scalar1=negmu[:, j : j + 1], scalar2=rstd[:, j : j + 1],
+                        op0=ALU.add, op1=ALU.mult,
+                    )
+
+            u = upool.tile([P, KB, SUP], BF16, name="u")
+            for kb in range(KB):
+                tp = ps_in.tile([P, 512], F32, tag="tin", name="tp")
+                for j in range(JT):
+                    nc.tensor.transpose(tp[:, P * j : P * (j + 1)], y[:, j, P * kb : P * (kb + 1)], ident[:])
+                nc.scalar.activation(
+                    out=u[:, kb, :], in_=tp[:], func=ACT.Identity,
+                    bias=cols[:, 8 + kb : 9 + kb], scale=cols[:, kb : kb + 1],
+                )
+
+            codes = cpool.tile([P, 2, SUP], U32, name="codes", align_bytes=64)
+            sc = cpool.tile([P, 2, SUP], U8, name="sc", align_bytes=64)
+            grps = []
+            for g in range(2):
+                grp = gpool.tile([P, SUP, 4], BF16, name="grp%d" % g, align_bytes=64)
+                nc.vector.tensor_copy(
+                    out=grp[:].rearrange("p (c i) t -> p c t i", i=4),
+                    in_=u[:, 4 * g : 4 * g + 4, :].rearrange("p t (c i) -> p c t i", i=4),
+                )
+                grps.append(grp)
+            for g in range(2):
+                nc.vector.quantize_mx(
+                    out=codes[:, g, :].bitcast(FP8X4),
+                    scales=sc[:, g, :],
+                    in_=grps[g][:].rearrange("p c t -> p (c t)"),
+                )
+
+            accs = []
+            for h in range(2):
+                acc = ps_acc.tile([P, SUP], F32, name="acc%d" % h)
+                for g in range(2):
+                    nc.tensor.matmul_mx(
+                        out=acc[:],
+                        lhsT=wcodes[:, 2 * h + g, :].bitcast(FP8X4),
+                        lhsT_scale=wsc[:, 2 * h + g, :],
+                        rhs=codes[:, g, :].bitcast(FP8X4),
+                        rhs_scale=sc[:, g, :],
+                        start=(g == 0),
+                        stop=(g == 1),
+                    )
+                accs.append(acc)
+
+            hgT = epool.tile([P, SUP], F32, name="hgT")
+            nc.scalar.activation(out=hgT[:], in_=accs[0][:], func=ACT.Silu, bias=cols[:, 16:17], scale=1.0)
+            zT = epool.tile([P, SUP], F32, name="zT")
+            nc.scalar.activation(out=zT[:], in_=accs[1][:], func=ACT.Silu, bias=cols[:, 17:18], scale=1.0)
+            qT = epool.tile([P, SUP], F32, name="qT")
+            nc.vector.tensor_scalar(
+                out=qT[:], in0=zT[:], scalar1=cols[:, 18:19], scalar2=cols[:, 20:21], op0=ALU.mult, op1=ALU.add
+            )
+            kT = epool.tile([P, SUP], F32, name="kT")
+            nc.vector.tensor_scalar(
+                out=kT[:], in0=zT[:], scalar1=cols[:, 19:20], scalar2=cols[:, 21:22], op0=ALU.mult, op1=ALU.add
+            )
+
+            ovg = opool.tile([P, 2, JT, 64], F32, name="ovg")
+            oq = opool.tile([P, JT, P], F32, name="oq")
+            ok = opool.tile([P, JT, P], F32, name="ok")
+            for i, (src, dst) in enumerate(((hgT, ovg), (qT, oq), (kT, ok))):
+                to = ps_out.tile([P, 512], F32, tag="tout", name="to")
+                for j in range(JT):
+                    nc.tensor.transpose(to[:, P * j : P * (j + 1)], src[:, P * j : P * (j + 1)], ident[:])
+                if i == 0:
+                    o_ap = dst[:]
+                    i_ap = to[:].rearrange("p (j h o) -> p h j o", j=JT, h=2)
+                else:
+                    o_ap = dst[:].rearrange("p j o -> p (j o)")
+                    i_ap = to[:]
+                if EVAC_ENGINE[i] == "s":
+                    nc.scalar.copy(out=o_ap, in_=i_ap)
+                else:
+                    nc.vector.tensor_copy(out=o_ap, in_=i_ap)
+
+            nc.sync.dma_start(
+                out=vf[r0 : r0 + SUP, :].rearrange("(p j) o -> p j o", j=JT), in_=ovg[:, 0, :, :]
+            )
+            nc.sync.dma_start(
+                out=gf[r0 : r0 + SUP, :].rearrange("(p j) o -> p j o", j=JT), in_=ovg[:, 1, :, :]
+            )
+            nc.sync.dma_start(out=qf[r0 : r0 + SUP, :].rearrange("(p j) o -> p j o", j=JT), in_=oq[:])
+            nc.sync.dma_start(out=kf[r0 : r0 + SUP, :].rearrange("(p j) o -> p j o", j=JT), in_=ok[:])

@@ -22,7 +22,6 @@ EPS = 1e-5
 FLOPS = 2 * ROWS * D * 256
 
 B_ENGINE = ("g", "g", "g", "s")
-EVAC_ENGINE = ("s", "s", "s")
 
 
 def tile_gau_pb_t_kernel(
@@ -30,12 +29,15 @@ def tile_gau_pb_t_kernel(
 ):
     nc = tc.nc
     xf = x.flatten_outer_dims()
-    vf = out_0.flatten_outer_dims()
-    gf = out_1.flatten_outer_dims()
-    qf = out_2.flatten_outer_dims()
-    kf = out_3.flatten_outer_dims()
+    outs = {
+        "v": out_0.flatten_outer_dims(),
+        "g": out_1.flatten_outer_dims(),
+        "q": out_2.flatten_outer_dims(),
+        "k": out_3.flatten_outer_dims(),
+    }
 
     with ExitStack() as ctx:
+        ctx.enter_context(tc.manual_schedule())
         keep = ctx.enter_context(tc.tile_pool(name="keep", bufs=1))
         xpool = ctx.enter_context(tc.tile_pool(name="xpool", bufs=4))
         small = ctx.enter_context(tc.tile_pool(name="small", bufs=4))
@@ -49,11 +51,15 @@ def tile_gau_pb_t_kernel(
         ps_acc = ctx.enter_context(tc.psum_pool(name="ps_acc", bufs=1))
         ps_out = ctx.enter_context(tc.psum_pool(name="ps_out", bufs=2))
 
+        T = {}
+
+        def valid(s):
+            return 0 <= s < NSUP
+
         ident = keep.tile([P, P], F32, name="ident")
         make_identity(nc, ident[:])
         mhalf = keep.tile([P, JT], F32, name="mhalf")
         nc.vector.memset(mhalf[:], -0.5)
-
         cst_b = keep.tile([P, P], BF16, name="cst_b")
         nc.vector.memset(cst_b[:], 0.0)
         nc.scalar.dma_start(out=cst_b[0:8, :], in_=ln_w.rearrange("(a b) -> a b", b=P))
@@ -62,40 +68,57 @@ def tile_gau_pb_t_kernel(
         nc.scalar.dma_start(out=cst_b[17:18, :], in_=b_qk.rearrange("(a b) -> a b", b=P))
         nc.scalar.dma_start(out=cst_b[18:20, :], in_=gamma)
         nc.scalar.dma_start(out=cst_b[20:22, :], in_=beta)
-        cst_f = keep.tile([P, P], F32, name="cst_f")
-        nc.vector.tensor_copy(out=cst_f[:], in_=cst_b[:])
-        tpc = ps_in.tile([P, 512], F32, tag="tin", name="tpc")
-        nc.tensor.transpose(tpc[:, 0:P], cst_f[:], ident[:])
-        cols = keep.tile([P, 32], F32, name="cols")
-        nc.vector.tensor_copy(out=cols[:, 0:22], in_=tpc[:, 0:22])
-
-        wgrp = keep.tile([P, 4, P, 4], BF16, name="wgrp", align_bytes=64)
-        wcodes = keep.tile([P, 4, P], U32, name="wcodes", align_bytes=64)
-        wsc = keep.tile([P, 4, P], U8, name="wsc", align_bytes=64)
+        wbs = []
         for h, W in enumerate((W_hidden, W_qk)):
             wb = keep.tile([P, D], BF16, name="wb%d" % h)
             nc.scalar.dma_start(out=wb[:], in_=W)
-            wf = keep.tile([P, D], F32, name="wf%d" % h)
-            nc.vector.tensor_copy(out=wf[:], in_=wb[:])
-            for g in range(2):
-                tpw = ps_in.tile([P, 512], F32, tag="tin", name="tpw")
-                for t in range(4):
-                    c0 = 512 * g + P * t
-                    nc.tensor.transpose(tpw[:, P * t : P * (t + 1)], wf[:, c0 : c0 + P], ident[:])
-                nc.vector.tensor_copy(
-                    out=wgrp[:, 2 * h + g, :, :], in_=tpw[:].rearrange("p (t o) -> p o t", t=4)
-                )
-        nc.vector.quantize_mx(
-            out=wcodes[:].rearrange("p a o -> p (a o)").bitcast(FP8X4),
-            scales=wsc[:].rearrange("p a o -> p (a o)"),
-            in_=wgrp[:].rearrange("p a o t -> p (a o t)"),
-        )
+            wbs.append(wb)
+        cols = keep.tile([P, 32], F32, name="cols")
+        wgrp = keep.tile([P, 4, P, 4], BF16, name="wgrp", align_bytes=64)
+        wcodes = keep.tile([P, 4, P], U32, name="wcodes", align_bytes=64)
+        wsc = keep.tile([P, 4, P], U8, name="wsc", align_bytes=64)
 
-        for s in range(NSUP):
-            r0 = SUP * s
+        def prep_consts():
+            cst_f = keep.tile([P, P], F32, name="cst_f")
+            nc.vector.tensor_copy(out=cst_f[:], in_=cst_b[:])
+            tpc = ps_in.tile([P, 512], F32, tag="tin", name="tpc")
+            nc.tensor.transpose(tpc[:, 0:P], cst_f[:], ident[:])
+            nc.vector.tensor_copy(out=cols[:, 0:22], in_=tpc[:, 0:22])
+
+        def prep_weights():
+            for h in range(2):
+                wf = keep.tile([P, D], F32, name="wf%d" % h)
+                nc.vector.tensor_copy(out=wf[:], in_=wbs[h][:])
+                for g in range(2):
+                    tpw = ps_in.tile([P, 512], F32, tag="tin", name="tpw")
+                    for t in range(4):
+                        c0 = 512 * g + P * t
+                        nc.tensor.transpose(tpw[:, P * t : P * (t + 1)], wf[:, c0 : c0 + P], ident[:])
+                    nc.vector.tensor_copy(
+                        out=wgrp[:, 2 * h + g, :, :], in_=tpw[:].rearrange("p (t o) -> p o t", t=4)
+                    )
+            nc.vector.quantize_mx(
+                out=wcodes[:].rearrange("p a o -> p (a o)").bitcast(FP8X4),
+                scales=wsc[:].rearrange("p a o -> p (a o)"),
+                in_=wgrp[:].rearrange("p a o t -> p (a o t)"),
+            )
+
+        def load(s):
+            if not valid(s):
+                return
             xs = xpool.tile([P, JT, D], BF16, name="xs")
-            nc.sync.dma_start(out=xs[:], in_=xf[r0 : r0 + SUP, :].rearrange("(p j) k -> p j k", j=JT))
+            T["xs", s] = xs
+            src = xf[SUP * s : SUP * (s + 1), :].rearrange("(p j) k -> p j k", j=JT)
+            if s == 0:
+                for j in range(JT):
+                    nc.sync.dma_start(out=xs[:, j, :], in_=src[:, j, :])
+            else:
+                nc.sync.dma_start(out=xs[:], in_=src)
 
+        def stats(s):
+            if not valid(s):
+                return
+            xs = T["xs", s]
             st = small.tile([P, JT, 2, 6], F32, name="st")
             mv = small.tile([P, JT, 2], F32, name="mv")
             for j in range(JT):
@@ -106,32 +129,61 @@ def tile_gau_pb_t_kernel(
             nc.vector.tensor_scalar_add(out=ve[:], in0=mv[:, :, 1], scalar1=EPS)
             negmu = small.tile([P, JT], F32, name="negmu")
             nc.vector.tensor_scalar_mul(out=negmu[:], in0=mv[:, :, 0], scalar1=-1.0)
-            rstd = small.tile([P, JT], F32, name="rstd")
-            nc.gpsimd.tensor_tensor(out=rstd[:], in0=ve[:], in1=mhalf[:], op=ALU.pow)
-            nmr = small.tile([P, JT], F32, name="nmr")
-            nc.vector.tensor_mul(out=nmr[:], in0=negmu[:], in1=rstd[:])
+            T["ve", s] = ve
+            T["negmu", s] = negmu
 
-            y = ypool.tile([P, JT, D], F32, name="y")
+        def rstd_stage(s):
+            if not valid(s):
+                return
+            rstd = small.tile([P, JT], F32, name="rstd")
+            nc.gpsimd.tensor_tensor(out=rstd[:], in0=T["ve", s][:], in1=mhalf[:], op=ALU.pow)
+            T["rstd", s] = rstd
+
+        def gate(s):
+            if not valid(s):
+                return
+            late = small.tile([P, JT], F32, name="late")
+            nc.vector.tensor_copy(out=late[:], in_=T["negmu", s][:])
+            T["late", s] = late
+            nmr = small.tile([P, JT], F32, name="nmr")
+            nc.vector.tensor_mul(out=nmr[:], in0=T["negmu", s][:], in1=T["rstd", s][:])
+            T["nmr", s] = nmr
+
+        def norm(s, eng):
+            if not valid(s):
+                return
+            if ("y", s) not in T:
+                T["y", s] = ypool.tile([P, JT, D], F32, name="y")
+            y = T["y", s]
+            xs = T["xs", s]
+            rstd = T["rstd", s]
             for j in range(JT):
-                if B_ENGINE[j] == "g":
+                if B_ENGINE[j] != eng:
+                    continue
+                if eng == "g":
                     nc.gpsimd.tensor_scalar(
                         out=y[:, j, :], in0=xs[:, j, :],
-                        scalar1=negmu[:, j : j + 1], scalar2=rstd[:, j : j + 1],
+                        scalar1=T["late", s][:, j : j + 1], scalar2=rstd[:, j : j + 1],
                         op0=ALU.add, op1=ALU.mult,
                     )
-                elif B_ENGINE[j] == "s":
+                elif eng == "s":
                     nc.scalar.activation(
                         out=y[:, j, :], in_=xs[:, j, :], func=ACT.Identity,
-                        bias=nmr[:, j : j + 1], scale=rstd[:, j : j + 1],
+                        bias=T["nmr", s][:, j : j + 1], scale=rstd[:, j : j + 1],
                     )
                 else:
                     nc.vector.tensor_scalar(
                         out=y[:, j, :], in0=xs[:, j, :],
-                        scalar1=negmu[:, j : j + 1], scalar2=rstd[:, j : j + 1],
+                        scalar1=T["negmu", s][:, j : j + 1], scalar2=rstd[:, j : j + 1],
                         op0=ALU.add, op1=ALU.mult,
                     )
 
+        def t1c(s):
+            if not valid(s):
+                return
+            y = T["y", s]
             u = upool.tile([P, KB, SUP], BF16, name="u")
+            T["u", s] = u
             for kb in range(KB):
                 tp = ps_in.tile([P, 512], F32, tag="tin", name="tp")
                 for j in range(JT):
@@ -141,8 +193,14 @@ def tile_gau_pb_t_kernel(
                     bias=cols[:, 8 + kb : 9 + kb], scale=cols[:, kb : kb + 1],
                 )
 
+        def regroup_quant(s):
+            if not valid(s):
+                return
+            u = T["u", s]
             codes = cpool.tile([P, 2, SUP], U32, name="codes", align_bytes=64)
             sc = cpool.tile([P, 2, SUP], U8, name="sc", align_bytes=64)
+            T["codes", s] = codes
+            T["sc", s] = sc
             grps = []
             for g in range(2):
                 grp = gpool.tile([P, SUP, 4], BF16, name="grp%d" % g, align_bytes=64)
@@ -158,9 +216,14 @@ def tile_gau_pb_t_kernel(
                     in_=grps[g][:].rearrange("p c t -> p (c t)"),
                 )
 
-            accs = []
+        def mx(s):
+            if not valid(s):
+                return
+            codes = T["codes", s]
+            sc = T["sc", s]
             for h in range(2):
                 acc = ps_acc.tile([P, SUP], F32, name="acc%d" % h)
+                T["acc%d" % h, s] = acc
                 for g in range(2):
                     nc.tensor.matmul_mx(
                         out=acc[:],
@@ -171,44 +234,91 @@ def tile_gau_pb_t_kernel(
                         start=(g == 0),
                         stop=(g == 1),
                     )
-                accs.append(acc)
 
+        def silu(s):
+            if not valid(s):
+                return
             hgT = epool.tile([P, SUP], F32, name="hgT")
-            nc.scalar.activation(out=hgT[:], in_=accs[0][:], func=ACT.Silu, bias=cols[:, 16:17], scale=1.0)
+            nc.scalar.activation(out=hgT[:], in_=T["acc0", s][:], func=ACT.Silu, bias=cols[:, 16:17], scale=1.0)
             zT = epool.tile([P, SUP], F32, name="zT")
-            nc.scalar.activation(out=zT[:], in_=accs[1][:], func=ACT.Silu, bias=cols[:, 17:18], scale=1.0)
-            qT = epool.tile([P, SUP], F32, name="qT")
-            nc.vector.tensor_scalar(
-                out=qT[:], in0=zT[:], scalar1=cols[:, 18:19], scalar2=cols[:, 20:21], op0=ALU.mult, op1=ALU.add
-            )
-            kT = epool.tile([P, SUP], F32, name="kT")
-            nc.vector.tensor_scalar(
-                out=kT[:], in0=zT[:], scalar1=cols[:, 19:20], scalar2=cols[:, 21:22], op0=ALU.mult, op1=ALU.add
-            )
+            nc.scalar.activation(out=zT[:], in_=T["acc1", s][:], func=ACT.Silu, bias=cols[:, 17:18], scale=1.0)
+            T["hg", s] = hgT
+            T["z", s] = zT
 
-            ovg = opool.tile([P, 2, JT, 64], F32, name="ovg")
-            oq = opool.tile([P, JT, P], F32, name="oq")
-            ok = opool.tile([P, JT, P], F32, name="ok")
-            for i, (src, dst) in enumerate(((hgT, ovg), (qT, oq), (kT, ok))):
-                to = ps_out.tile([P, 512], F32, tag="tout", name="to")
-                for j in range(JT):
-                    nc.tensor.transpose(to[:, P * j : P * (j + 1)], src[:, P * j : P * (j + 1)], ident[:])
-                if i == 0:
-                    o_ap = dst[:]
-                    i_ap = to[:].rearrange("p (j h o) -> p h j o", j=JT, h=2)
-                else:
-                    o_ap = dst[:].rearrange("p j o -> p (j o)")
-                    i_ap = to[:]
-                if EVAC_ENGINE[i] == "s":
-                    nc.scalar.copy(out=o_ap, in_=i_ap)
-                else:
-                    nc.vector.tensor_copy(out=o_ap, in_=i_ap)
+        def qk(s):
+            if not valid(s):
+                return
+            zT = T["z", s]
+            for i, nm in enumerate(("q", "k")):
+                t = epool.tile([P, SUP], F32, name=nm + "T")
+                nc.vector.tensor_scalar(
+                    out=t[:], in0=zT[:], scalar1=cols[:, 18 + i : 19 + i], scalar2=cols[:, 20 + i : 21 + i],
+                    op0=ALU.mult, op1=ALU.add,
+                )
+                T[nm, s] = t
 
-            nc.sync.dma_start(
-                out=vf[r0 : r0 + SUP, :].rearrange("(p j) o -> p j o", j=JT), in_=ovg[:, 0, :, :]
-            )
-            nc.sync.dma_start(
-                out=gf[r0 : r0 + SUP, :].rearrange("(p j) o -> p j o", j=JT), in_=ovg[:, 1, :, :]
-            )
-            nc.sync.dma_start(out=qf[r0 : r0 + SUP, :].rearrange("(p j) o -> p j o", j=JT), in_=oq[:])
-            nc.sync.dma_start(out=kf[r0 : r0 + SUP, :].rearrange("(p j) o -> p j o", j=JT), in_=ok[:])
+        def t2(s, nm):
+            if not valid(s):
+                return
+            src = T[nm, s]
+            to = ps_out.tile([P, 512], F32, tag="tout", name="to_" + nm)
+            T["to_" + nm, s] = to
+            for j in range(JT):
+                nc.tensor.transpose(to[:, P * j : P * (j + 1)], src[:, P * j : P * (j + 1)], ident[:])
+
+        def evac(s, nm, eng="s"):
+            if not valid(s):
+                return
+            to = T["to_" + nm, s]
+            if nm == "hg":
+                dst = opool.tile([P, 2, JT, 64], F32, name="o_hg")
+                o_ap = dst[:]
+                i_ap = to[:].rearrange("p (j h o) -> p h j o", j=JT, h=2)
+            else:
+                dst = opool.tile([P, JT, P], F32, name="o_" + nm)
+                o_ap = dst[:].rearrange("p j o -> p (j o)")
+                i_ap = to[:]
+            T["o_" + nm, s] = dst
+            if eng == "s":
+                nc.scalar.copy(out=o_ap, in_=i_ap)
+            else:
+                nc.vector.tensor_copy(out=o_ap, in_=i_ap)
+
+        def store(s, nm):
+            if not valid(s):
+                return
+            rows = slice(SUP * s, SUP * (s + 1))
+            if nm == "hg":
+                o = T["o_hg", s]
+                nc.sync.dma_start(out=outs["v"][rows, :].rearrange("(p j) o -> p j o", j=JT), in_=o[:, 0, :, :])
+                nc.sync.dma_start(out=outs["g"][rows, :].rearrange("(p j) o -> p j o", j=JT), in_=o[:, 1, :, :])
+            else:
+                nc.sync.dma_start(out=outs[nm][rows, :].rearrange("(p j) o -> p j o", j=JT), in_=T["o_" + nm, s][:])
+
+        load(0)
+        load(1)
+        for i in range(NSUP + 5):
+            load(i + 2)
+            stats(i)
+            if i == 0:
+                prep_consts()
+            if i == 1:
+                prep_weights()
+            norm(i - 1, "g")
+            rstd_stage(i)
+            mx(i - 3)
+            t2(i - 4, "q")
+            t2(i - 4, "k")
+            silu(i - 3)
+            t2(i - 3, "hg")
+            evac(i - 4, "q")
+            evac(i - 4, "k")
+            store(i - 4, "q")
+            store(i - 4, "k")
+            evac(i - 3, "hg")
+            store(i - 3, "hg")
+            norm(i - 1, "s")
+            t1c(i - 1)
+            regroup_quant(i - 2)
+            qk(i - 3)
+            gate(i)

@@ -47,9 +47,9 @@ def tile_gau_pb_t_kernel(
         cpool = ctx.enter_context(tc.tile_pool(name="cpool", bufs=2))
         epool = ctx.enter_context(tc.tile_pool(name="epool", bufs=2))
         opool = ctx.enter_context(tc.tile_pool(name="opool", bufs=2))
-        ps_in = ctx.enter_context(tc.psum_pool(name="ps_in", bufs=4))
+        ps_in = ctx.enter_context(tc.psum_pool(name="ps_in", bufs=3))
         ps_acc = ctx.enter_context(tc.psum_pool(name="ps_acc", bufs=1))
-        ps_out = ctx.enter_context(tc.psum_pool(name="ps_out", bufs=2))
+        ps_out = ctx.enter_context(tc.psum_pool(name="ps_out", bufs=3))
 
         T = {}
 
@@ -80,23 +80,25 @@ def tile_gau_pb_t_kernel(
 
         def prep_consts():
             cst_f = keep.tile([P, P], F32, name="cst_f")
-            nc.vector.tensor_copy(out=cst_f[:], in_=cst_b[:])
+            nc.scalar.copy(out=cst_f[:], in_=cst_b[:])
             tpc = ps_in.tile([P, 512], F32, tag="tin", name="tpc")
             nc.tensor.transpose(tpc[:, 0:P], cst_f[:], ident[:])
-            nc.vector.tensor_copy(out=cols[:, 0:22], in_=tpc[:, 0:22])
+            nc.scalar.copy(out=cols[:, 0:22], in_=tpc[:, 0:22])
 
         def prep_weights():
             for h in range(2):
                 wf = keep.tile([P, D], F32, name="wf%d" % h)
-                nc.vector.tensor_copy(out=wf[:], in_=wbs[h][:])
+                nc.scalar.copy(out=wf[:], in_=wbs[h][:])
                 for g in range(2):
                     tpw = ps_in.tile([P, 512], F32, tag="tin", name="tpw")
                     for t in range(4):
                         c0 = 512 * g + P * t
                         nc.tensor.transpose(tpw[:, P * t : P * (t + 1)], wf[:, c0 : c0 + P], ident[:])
-                    nc.vector.tensor_copy(
+                    nc.scalar.copy(
                         out=wgrp[:, 2 * h + g, :, :], in_=tpw[:].rearrange("p (t o) -> p o t", t=4)
                     )
+
+        def quant_weights():
             nc.vector.quantize_mx(
                 out=wcodes[:].rearrange("p a o -> p (a o)").bitcast(FP8X4),
                 scales=wsc[:].rearrange("p a o -> p (a o)"),
@@ -145,8 +147,12 @@ def tile_gau_pb_t_kernel(
             late = small.tile([P, JT], F32, name="late")
             nc.vector.tensor_copy(out=late[:], in_=T["negmu", s][:])
             T["late", s] = late
+
+        def nmr_stage(s):
+            if not valid(s):
+                return
             nmr = small.tile([P, JT], F32, name="nmr")
-            nc.vector.tensor_mul(out=nmr[:], in0=T["negmu", s][:], in1=T["rstd", s][:])
+            nc.gpsimd.tensor_tensor(out=nmr[:], in0=T["late", s][:], in1=T["rstd", s][:], op=ALU.mult)
             T["nmr", s] = nmr
 
         def norm(s, eng):
@@ -297,15 +303,17 @@ def tile_gau_pb_t_kernel(
 
         load(0)
         load(1)
+        prep_consts()
+        prep_weights()
         for i in range(NSUP + 5):
             load(i + 2)
             stats(i)
-            if i == 0:
-                prep_consts()
             if i == 1:
-                prep_weights()
+                quant_weights()
+            nmr_stage(i - 1)
             norm(i - 1, "g")
             rstd_stage(i)
+            norm(i - 1, "s")
             mx(i - 3)
             t2(i - 4, "q")
             t2(i - 4, "k")
@@ -317,7 +325,6 @@ def tile_gau_pb_t_kernel(
             store(i - 4, "k")
             evac(i - 3, "hg")
             store(i - 3, "hg")
-            norm(i - 1, "s")
             t1c(i - 1)
             regroup_quant(i - 2)
             qk(i - 3)

@@ -37,7 +37,6 @@ def tile_gau_pb_t_kernel(
     }
 
     with ExitStack() as ctx:
-        ctx.enter_context(tc.manual_schedule())
         keep = ctx.enter_context(tc.tile_pool(name="keep", bufs=1))
         xpool = ctx.enter_context(tc.tile_pool(name="xpool", bufs=4))
         small = ctx.enter_context(tc.tile_pool(name="small", bufs=4))

@@ -21,7 +21,7 @@ KB = D // P
 EPS = 1e-5
 FLOPS = 2 * ROWS * D * 256
 
-B_ENGINE = ("g", "g", "g", "s")
+B_ENGINE = ("g", "g", "g", "v")
 
 
 def tile_gau_pb_t_kernel(
@@ -309,10 +309,8 @@ def tile_gau_pb_t_kernel(
             stats(i)
             if i == 1:
                 quant_weights()
-            nmr_stage(i - 1)
             norm(i - 1, "g")
             rstd_stage(i)
-            norm(i - 1, "s")
             mx(i - 3)
             t2(i - 4, "q")
             t2(i - 4, "k")
@@ -328,3 +326,4 @@ def tile_gau_pb_t_kernel(
             regroup_quant(i - 2)
             qk(i - 3)
             gate(i)
+            norm(i, "v")

@@ -21,7 +21,7 @@ KB = D // P
 EPS = 1e-5
 FLOPS = 2 * ROWS * D * 256
 
-B_ENGINE = ("g", "g", "g", "v")
+B_ENGINE = ("g", "g", "g", "s")
 
 
 def tile_gau_pb_t_kernel(
@@ -37,6 +37,7 @@ def tile_gau_pb_t_kernel(
     }
 
     with ExitStack() as ctx:
+        ctx.enter_context(tc.manual_schedule())
         keep = ctx.enter_context(tc.tile_pool(name="keep", bufs=1))
         xpool = ctx.enter_context(tc.tile_pool(name="xpool", bufs=4))
         small = ctx.enter_context(tc.tile_pool(name="small", bufs=4))
@@ -256,9 +257,9 @@ def tile_gau_pb_t_kernel(
             zT = T["z", s]
             for i, nm in enumerate(("q", "k")):
                 t = epool.tile([P, SUP], F32, name=nm + "T")
-                nc.vector.tensor_scalar(
-                    out=t[:], in0=zT[:], scalar1=cols[:, 18 + i : 19 + i], scalar2=cols[:, 20 + i : 21 + i],
-                    op0=ALU.mult, op1=ALU.add,
+                nc.scalar.activation(
+                    out=t[:], in_=zT[:], func=ACT.Identity,
+                    bias=cols[:, 20 + i : 21 + i], scale=cols[:, 18 + i : 19 + i],
                 )
                 T[nm, s] = t
 
@@ -309,8 +310,10 @@ def tile_gau_pb_t_kernel(
             stats(i)
             if i == 1:
                 quant_weights()
+            nmr_stage(i - 1)
             norm(i - 1, "g")
             rstd_stage(i)
+            norm(i - 1, "s")
             mx(i - 3)
             t2(i - 4, "q")
             t2(i - 4, "k")
@@ -323,7 +326,6 @@ def tile_gau_pb_t_kernel(
             evac(i - 3, "hg")
             store(i - 3, "hg")
             t1c(i - 1)
-            regroup_quant(i - 2)
             qk(i - 3)
+            regroup_quant(i - 2)
             gate(i)
-            norm(i, "v")

@@ -127,32 +127,31 @@ def tile_gau_pb_t_kernel(
                 for c in range(2):
                     nc.vector.bn_stats(out=st[:, j, c, :], in_=xs[:, j, 512 * c : 512 * (c + 1)])
                 nc.vector.bn_aggr(out=mv[:, j, :], in_=st[:, j, :, :].rearrange("p c v -> p (c v)"))
-            ve = small.tile([P, JT], F32, name="ve")
-            nc.vector.tensor_scalar_add(out=ve[:], in0=mv[:, :, 1], scalar1=EPS)
-            negmu = small.tile([P, JT], F32, name="negmu")
-            nc.vector.tensor_scalar_mul(out=negmu[:], in0=mv[:, :, 0], scalar1=-1.0)
-            T["ve", s] = ve
-            T["negmu", s] = negmu
+            T["mv", s] = mv
 
         def rstd_stage(s):
             if not valid(s):
                 return
+            ve = small.tile([P, JT], F32, name="ve")
+            nc.gpsimd.tensor_scalar(
+                out=ve[:], in0=T["mv", s][:, :, 1], scalar1=EPS, scalar2=1.0, op0=ALU.add, op1=ALU.mult
+            )
             rstd = small.tile([P, JT], F32, name="rstd")
-            nc.gpsimd.tensor_tensor(out=rstd[:], in0=T["ve", s][:], in1=mhalf[:], op=ALU.pow)
+            nc.gpsimd.tensor_tensor(out=rstd[:], in0=ve[:], in1=mhalf[:], op=ALU.pow)
             T["rstd", s] = rstd
 
         def gate(s):
             if not valid(s):
                 return
-            late = small.tile([P, JT], F32, name="late")
-            nc.vector.tensor_copy(out=late[:], in_=T["negmu", s][:])
-            T["late", s] = late
+            negmu = small.tile([P, JT], F32, name="negmu")
+            nc.vector.tensor_scalar_mul(out=negmu[:], in0=T["mv", s][:, :, 0], scalar1=-1.0)
+            T["negmu", s] = negmu
 
         def nmr_stage(s):
             if not valid(s):
                 return
             nmr = small.tile([P, JT], F32, name="nmr")
-            nc.gpsimd.tensor_tensor(out=nmr[:], in0=T["late", s][:], in1=T["rstd", s][:], op=ALU.mult)
+            nc.gpsimd.tensor_tensor(out=nmr[:], in0=T["negmu", s][:], in1=T["rstd", s][:], op=ALU.mult)
             T["nmr", s] = nmr
 
         def norm(s, eng):
@@ -169,7 +168,7 @@ def tile_gau_pb_t_kernel(
                 if eng == "g":
                     nc.gpsimd.tensor_scalar(
                         out=y[:, j, :], in0=xs[:, j, :],
-                        scalar1=T["late", s][:, j : j + 1], scalar2=rstd[:, j : j + 1],
+                        scalar1=T["negmu", s][:, j : j + 1], scalar2=rstd[:, j : j + 1],
                         op0=ALU.add, op1=ALU.mult,
                     )
                 elif eng == "s":
@@ -199,28 +198,29 @@ def tile_gau_pb_t_kernel(
                     bias=cols[:, 8 + kb : 9 + kb], scale=cols[:, kb : kb + 1],
                 )
 
-        def regroup_quant(s):
+        def regroup(s):
             if not valid(s):
                 return
-            u = T["u", s]
+            grp = gpool.tile([P, 2, SUP, 4], BF16, name="grp", align_bytes=64)
+            T["grp", s] = grp
+            nc.vector.tensor_copy(
+                out=grp[:].rearrange("p g (c i) t -> p g c t i", i=4),
+                in_=T["u", s][:].rearrange("p (g t) (c i) -> p g c t i", g=2, i=4),
+            )
+
+        def quantise(s):
+            if not valid(s):
+                return
+            grp = T["grp", s]
             codes = cpool.tile([P, 2, SUP], U32, name="codes", align_bytes=64)
             sc = cpool.tile([P, 2, SUP], U8, name="sc", align_bytes=64)
             T["codes", s] = codes
             T["sc", s] = sc
-            grps = []
-            for g in range(2):
-                grp = gpool.tile([P, SUP, 4], BF16, name="grp%d" % g, align_bytes=64)
-                nc.vector.tensor_copy(
-                    out=grp[:].rearrange("p (c i) t -> p c t i", i=4),
-                    in_=u[:, 4 * g : 4 * g + 4, :].rearrange("p t (c i) -> p c t i", i=4),
-                )
-                grps.append(grp)
-            for g in range(2):
-                nc.vector.quantize_mx(
-                    out=codes[:, g, :].bitcast(FP8X4),
-                    scales=sc[:, g, :],
-                    in_=grps[g][:].rearrange("p c t -> p (c t)"),
-                )
+            nc.vector.quantize_mx(
+                out=codes[:].rearrange("p g c -> p (g c)").bitcast(FP8X4),
+                scales=sc[:].rearrange("p g c -> p (g c)"),
+                in_=grp[:].rearrange("p g c t -> p (g c t)"),
+            )
 
         def mx(s):
             if not valid(s):
@@ -251,17 +251,24 @@ def tile_gau_pb_t_kernel(
             T["hg", s] = hgT
             T["z", s] = zT
 
-        def qk(s):
+        def scale_q(s):
             if not valid(s):
                 return
-            zT = T["z", s]
-            for i, nm in enumerate(("q", "k")):
-                t = epool.tile([P, SUP], F32, name=nm + "T")
-                nc.scalar.activation(
-                    out=t[:], in_=zT[:], func=ACT.Identity,
-                    bias=cols[:, 20 + i : 21 + i], scale=cols[:, 18 + i : 19 + i],
-                )
-                T[nm, s] = t
+            t = epool.tile([P, SUP], F32, name="qT")
+            nc.vector.tensor_scalar(
+                out=t[:], in0=T["z", s][:], scalar1=cols[:, 18:19], scalar2=cols[:, 20:21],
+                op0=ALU.mult, op1=ALU.add,
+            )
+            T["q", s] = t
+
+        def scale_k(s):
+            if not valid(s):
+                return
+            t = epool.tile([P, SUP], F32, name="kT")
+            nc.scalar.activation(
+                out=t[:], in_=T["z", s][:], func=ACT.Identity, bias=cols[:, 21:22], scale=cols[:, 19:20]
+            )
+            T["k", s] = t
 
         def t2(s, nm):
             if not valid(s):
@@ -326,6 +333,8 @@ def tile_gau_pb_t_kernel(
             evac(i - 3, "hg")
             store(i - 3, "hg")
             t1c(i - 1)
-            qk(i - 3)
-            regroup_quant(i - 2)
+            scale_k(i - 3)
+            regroup(i - 2)
+            scale_q(i - 3)
+            quantise(i - 2)
             gate(i)

@@ -128,16 +128,15 @@ def tile_gau_pb_t_kernel(
                     nc.vector.bn_stats(out=st[:, j, c, :], in_=xs[:, j, 512 * c : 512 * (c + 1)])
                 nc.vector.bn_aggr(out=mv[:, j, :], in_=st[:, j, :, :].rearrange("p c v -> p (c v)"))
             T["mv", s] = mv
+            ve = small.tile([P, JT], F32, name="ve")
+            nc.vector.tensor_scalar_add(out=ve[:], in0=mv[:, :, 1], scalar1=EPS)
+            T["ve", s] = ve
 
         def rstd_stage(s):
             if not valid(s):
                 return
-            ve = small.tile([P, JT], F32, name="ve")
-            nc.gpsimd.tensor_scalar(
-                out=ve[:], in0=T["mv", s][:, :, 1], scalar1=EPS, scalar2=1.0, op0=ALU.add, op1=ALU.mult
-            )
             rstd = small.tile([P, JT], F32, name="rstd")
-            nc.gpsimd.tensor_tensor(out=rstd[:], in0=ve[:], in1=mhalf[:], op=ALU.pow)
+            nc.gpsimd.tensor_tensor(out=rstd[:], in0=T["ve", s][:], in1=mhalf[:], op=ALU.pow)
             T["rstd", s] = rstd
 
         def gate(s):
@@ -146,12 +145,8 @@ def tile_gau_pb_t_kernel(
             negmu = small.tile([P, JT], F32, name="negmu")
             nc.vector.tensor_scalar_mul(out=negmu[:], in0=T["mv", s][:, :, 0], scalar1=-1.0)
             T["negmu", s] = negmu
-
-        def nmr_stage(s):
-            if not valid(s):
-                return
             nmr = small.tile([P, JT], F32, name="nmr")
-            nc.gpsimd.tensor_tensor(out=nmr[:], in0=T["negmu", s][:], in1=T["rstd", s][:], op=ALU.mult)
+            nc.vector.tensor_mul(out=nmr[:], in0=negmu[:], in1=T["rstd", s][:])
             T["nmr", s] = nmr
 
         def norm(s, eng):
@@ -317,7 +312,6 @@ def tile_gau_pb_t_kernel(
             stats(i)
             if i == 1:
                 quant_weights()
-            nmr_stage(i - 1)
             norm(i - 1, "g")
             rstd_stage(i)
             norm(i - 1, "s")

from contextlib import ExitStack

import concourse.mybir as mybir
from concourse.masks import make_identity

F32 = mybir.dt.float32
BF16 = mybir.dt.bfloat16
U32 = mybir.dt.uint32
U8 = mybir.dt.uint8
FP8X4 = mybir.dt.float8_e4m3fn_x4
ALU = mybir.AluOpType
ACT = mybir.ActivationFunctionType

P = 128
D = 1024
ROWS = 8192
JT = 4
SUP = P * JT
NSUP = ROWS // SUP
KB = D // P
EPS = 1e-5
FLOPS = 2 * ROWS * D * 256

B_ENGINE = ("g", "g", "g", "s")


def tile_gau_pb_t_kernel(
    tc, x, ln_w, ln_b, W_hidden, b_hidden, W_qk, b_qk, gamma, beta, out_0, out_1, out_2, out_3
):
    nc = tc.nc
    xf = x.flatten_outer_dims()
    outs = {
        "v": out_0.flatten_outer_dims(),
        "g": out_1.flatten_outer_dims(),
        "q": out_2.flatten_outer_dims(),
        "k": out_3.flatten_outer_dims(),
    }

    with ExitStack() as ctx:
        ctx.enter_context(tc.manual_schedule())
        keep = ctx.enter_context(tc.tile_pool(name="keep", bufs=1))
        xpool = ctx.enter_context(tc.tile_pool(name="xpool", bufs=4))
        small = ctx.enter_context(tc.tile_pool(name="small", bufs=4))
        ypool = ctx.enter_context(tc.tile_pool(name="ypool", bufs=2))
        upool = ctx.enter_context(tc.tile_pool(name="upool", bufs=2))
        gpool = ctx.enter_context(tc.tile_pool(name="gpool", bufs=2))
        cpool = ctx.enter_context(tc.tile_pool(name="cpool", bufs=2))
        epool = ctx.enter_context(tc.tile_pool(name="epool", bufs=2))
        opool = ctx.enter_context(tc.tile_pool(name="opool", bufs=2))
        ps_in = ctx.enter_context(tc.psum_pool(name="ps_in", bufs=3))
        ps_acc = ctx.enter_context(tc.psum_pool(name="ps_acc", bufs=1))
        ps_out = ctx.enter_context(tc.psum_pool(name="ps_out", bufs=3))

        T = {}

        def valid(s):
            return 0 <= s < NSUP

        ident = keep.tile([P, P], F32, name="ident")
        make_identity(nc, ident[:])
        mhalf = keep.tile([P, JT], F32, name="mhalf")
        nc.vector.memset(mhalf[:], -0.5)
        cst_b = keep.tile([P, P], BF16, name="cst_b")
        nc.vector.memset(cst_b[:], 0.0)
        nc.scalar.dma_start(out=cst_b[0:8, :], in_=ln_w.rearrange("(a b) -> a b", b=P))
        nc.scalar.dma_start(out=cst_b[8:16, :], in_=ln_b.rearrange("(a b) -> a b", b=P))
        nc.scalar.dma_start(out=cst_b[16:17, :], in_=b_hidden.rearrange("(a b) -> a b", b=P))
        nc.scalar.dma_start(out=cst_b[17:18, :], in_=b_qk.rearrange("(a b) -> a b", b=P))
        nc.scalar.dma_start(out=cst_b[18:20, :], in_=gamma)
        nc.scalar.dma_start(out=cst_b[20:22, :], in_=beta)
        wbs = []
        for h, W in enumerate((W_hidden, W_qk)):
            wb = keep.tile([P, D], BF16, name="wb%d" % h)
            nc.scalar.dma_start(out=wb[:], in_=W)
            wbs.append(wb)
        cols = keep.tile([P, 32], F32, name="cols")
        wgrp = keep.tile([P, 4, P, 4], BF16, name="wgrp", align_bytes=64)
        wcodes = keep.tile([P, 4, P], U32, name="wcodes", align_bytes=64)
        wsc = keep.tile([P, 4, P], U8, name="wsc", align_bytes=64)

        def prep_consts():
            cst_f = keep.tile([P, P], F32, name="cst_f")
            nc.scalar.copy(out=cst_f[:], in_=cst_b[:])
            tpc = ps_in.tile([P, 512], F32, tag="tin", name="tpc")
            nc.tensor.transpose(tpc[:, 0:P], cst_f[:], ident[:])
            nc.scalar.copy(out=cols[:, 0:22], in_=tpc[:, 0:22])

        def prep_weights():
            for h in range(2):
                wf = keep.tile([P, D], F32, name="wf%d" % h)
                nc.scalar.copy(out=wf[:], in_=wbs[h][:])
                for g in range(2):
                    tpw = ps_in.tile([P, 512], F32, tag="tin", name="tpw")
                    for t in range(4):
                        c0 = 512 * g + P * t
                        nc.tensor.transpose(tpw[:, P * t : P * (t + 1)], wf[:, c0 : c0 + P], ident[:])
                    nc.scalar.copy(
                        out=wgrp[:, 2 * h + g, :, :], in_=tpw[:].rearrange("p (t o) -> p o t", t=4)
                    )

        def quant_weights():
            nc.vector.quantize_mx(
                out=wcodes[:].rearrange("p a o -> p (a o)").bitcast(FP8X4),
                scales=wsc[:].rearrange("p a o -> p (a o)"),
                in_=wgrp[:].rearrange("p a o t -> p (a o t)"),
            )

        def load(s):
            if not valid(s):
                return
            xs = xpool.tile([P, JT, D], BF16, name="xs")
            T["xs", s] = xs
            src = xf[SUP * s : SUP * (s + 1), :].rearrange("(p j) k -> p j k", j=JT)
            if s == 0:
                for j in range(JT):
                    nc.sync.dma_start(out=xs[:, j, :], in_=src[:, j, :])
            else:
                nc.sync.dma_start(out=xs[:], in_=src)

        def stats(s):
            if not valid(s):
                return
            xs = T["xs", s]
            st = small.tile([P, JT, 2, 6], F32, name="st")
            mv = small.tile([P, JT, 2], F32, name="mv")
            for j in range(JT):
                for c in range(2):
                    nc.vector.bn_stats(out=st[:, j, c, :], in_=xs[:, j, 512 * c : 512 * (c + 1)])
                nc.vector.bn_aggr(out=mv[:, j, :], in_=st[:, j, :, :].rearrange("p c v -> p (c v)"))
            T["mv", s] = mv
            ve = small.tile([P, JT], F32, name="ve")
            nc.vector.tensor_scalar_add(out=ve[:], in0=mv[:, :, 1], scalar1=EPS)
            T["ve", s] = ve

        def rstd_stage(s):
            if not valid(s):
                return
            rstd = small.tile([P, JT], F32, name="rstd")
            nc.gpsimd.tensor_tensor(out=rstd[:], in0=T["ve", s][:], in1=mhalf[:], op=ALU.pow)
            T["rstd", s] = rstd

        def gate(s):
            if not valid(s):
                return
            negmu = small.tile([P, JT], F32, name="negmu")
            nc.vector.tensor_scalar_mul(out=negmu[:], in0=T["mv", s][:, :, 0], scalar1=-1.0)
            T["negmu", s] = negmu
            nmr = small.tile([P, JT], F32, name="nmr")
            nc.vector.tensor_mul(out=nmr[:], in0=negmu[:], in1=T["rstd", s][:])
            T["nmr", s] = nmr

        def norm(s, eng):
            if not valid(s):
                return
            if ("y", s) not in T:
                T["y", s] = ypool.tile([P, JT, D], F32, name="y")
            y = T["y", s]
            xs = T["xs", s]
            rstd = T["rstd", s]
            for j in range(JT):
                if B_ENGINE[j] != eng:
                    continue
                if eng == "g":
                    nc.gpsimd.tensor_scalar(
                        out=y[:, j, :], in0=xs[:, j, :],
                        scalar1=T["negmu", s][:, j : j + 1], scalar2=rstd[:, j : j + 1],
                        op0=ALU.add, op1=ALU.mult,
                    )
                elif eng == "s":
                    nc.scalar.activation(
                        out=y[:, j, :], in_=xs[:, j, :], func=ACT.Identity,
                        bias=T["nmr", s][:, j : j + 1], scale=rstd[:, j : j + 1],
                    )
                else:
                    nc.vector.tensor_scalar(
                        out=y[:, j, :], in0=xs[:, j, :],
                        scalar1=T["negmu", s][:, j : j + 1], scalar2=rstd[:, j : j + 1],
                        op0=ALU.add, op1=ALU.mult,
                    )

        def t1c(s):
            if not valid(s):
                return
            y = T["y", s]
            u = upool.tile([P, KB, SUP], BF16, name="u")
            T["u", s] = u
            for kb in range(KB):
                tp = ps_in.tile([P, 512], F32, tag="tin", name="tp")
                for j in range(JT):
                    nc.tensor.transpose(tp[:, P * j : P * (j + 1)], y[:, j, P * kb : P * (kb + 1)], ident[:])
                nc.scalar.activation(
                    out=u[:, kb, :], in_=tp[:], func=ACT.Identity,
                    bias=cols[:, 8 + kb : 9 + kb], scale=cols[:, kb : kb + 1],
                )

        def regroup(s):
            if not valid(s):
                return
            grp = gpool.tile([P, 2, SUP, 4], BF16, name="grp", align_bytes=64)
            T["grp", s] = grp
            nc.vector.tensor_copy(
                out=grp[:].rearrange("p g (c i) t -> p g c t i", i=4),
                in_=T["u", s][:].rearrange("p (g t) (c i) -> p g c t i", g=2, i=4),
            )

        def quantise(s):
            if not valid(s):
                return
            grp = T["grp", s]
            codes = cpool.tile([P, 2, SUP], U32, name="codes", align_bytes=64)
            sc = cpool.tile([P, 2, SUP], U8, name="sc", align_bytes=64)
            T["codes", s] = codes
            T["sc", s] = sc
            nc.vector.quantize_mx(
                out=codes[:].rearrange("p g c -> p (g c)").bitcast(FP8X4),
                scales=sc[:].rearrange("p g c -> p (g c)"),
                in_=grp[:].rearrange("p g c t -> p (g c t)"),
            )

        def mx(s):
            if not valid(s):
                return
            codes = T["codes", s]
            sc = T["sc", s]
            for h in range(2):
                acc = ps_acc.tile([P, SUP], F32, name="acc%d" % h)
                T["acc%d" % h, s] = acc
                for g in range(2):
                    nc.tensor.matmul_mx(
                        out=acc[:],
                        lhsT=wcodes[:, 2 * h + g, :].bitcast(FP8X4),
                        lhsT_scale=wsc[:, 2 * h + g, :],
                        rhs=codes[:, g, :].bitcast(FP8X4),
                        rhs_scale=sc[:, g, :],
                        start=(g == 0),
                        stop=(g == 1),
                    )

        def silu(s):
            if not valid(s):
                return
            hgT = epool.tile([P, SUP], F32, name="hgT")
            nc.scalar.activation(out=hgT[:], in_=T["acc0", s][:], func=ACT.Silu, bias=cols[:, 16:17], scale=1.0)
            zT = epool.tile([P, SUP], F32, name="zT")
            nc.scalar.activation(out=zT[:], in_=T["acc1", s][:], func=ACT.Silu, bias=cols[:, 17:18], scale=1.0)
            T["hg", s] = hgT
            T["z", s] = zT

        def scale_q(s):
            if not valid(s):
                return
            t = epool.tile([P, SUP], F32, name="qT")
            nc.vector.tensor_scalar(
                out=t[:], in0=T["z", s][:], scalar1=cols[:, 18:19], scalar2=cols[:, 20:21],
                op0=ALU.mult, op1=ALU.add,
            )
            T["q", s] = t

        def scale_k(s):
            if not valid(s):
                return
            t = epool.tile([P, SUP], F32, name="kT")
            nc.scalar.activation(
                out=t[:], in_=T["z", s][:], func=ACT.Identity, bias=cols[:, 21:22], scale=cols[:, 19:20]
            )
            T["k", s] = t

        def t2(s, nm):
            if not valid(s):
                return
            src = T[nm, s]
            to = ps_out.tile([P, 512], F32, tag="tout", name="to_" + nm)
            T["to_" + nm, s] = to
            for j in range(JT):
                nc.tensor.transpose(to[:, P * j : P * (j + 1)], src[:, P * j : P * (j + 1)], ident[:])

        def evac(s, nm, eng="s"):
            if not valid(s):
                return
            to = T["to_" + nm, s]
            if nm == "hg":
                dst = opool.tile([P, 2, JT, 64], F32, name="o_hg")
                o_ap = dst[:]
                i_ap = to[:].rearrange("p (j h o) -> p h j o", j=JT, h=2)
            else:
                dst = opool.tile([P, JT, P], F32, name="o_" + nm)
                o_ap = dst[:].rearrange("p j o -> p (j o)")
                i_ap = to[:]
            T["o_" + nm, s] = dst
            if eng == "s":
                nc.scalar.copy(out=o_ap, in_=i_ap)
            else:
                nc.vector.tensor_copy(out=o_ap, in_=i_ap)

        def store(s, nm):
            if not valid(s):
                return
            rows = slice(SUP * s, SUP * (s + 1))
            if nm == "hg":
                o = T["o_hg", s]
                nc.sync.dma_start(out=outs["v"][rows, :].rearrange("(p j) o -> p j o", j=JT), in_=o[:, 0, :, :])
                nc.sync.dma_start(out=outs["g"][rows, :].rearrange("(p j) o -> p j o", j=JT), in_=o[:, 1, :, :])
            else:
                nc.sync.dma_start(out=outs[nm][rows, :].rearrange("(p j) o -> p j o", j=JT), in_=T["o_" + nm, s][:])

        load(0)
        load(1)
        prep_consts()
        prep_weights()
        for i in range(NSUP + 5):
            load(i + 2)
            stats(i)
            if i == 1:
                quant_weights()
            norm(i - 1, "g")
            rstd_stage(i)
            norm(i - 1, "s")
            mx(i - 3)
            t2(i - 4, "q")
            t2(i - 4, "k")
            silu(i - 3)
            t2(i - 3, "hg")
            evac(i - 4, "q")
            evac(i - 4, "k")
            store(i - 4, "q")
            store(i - 4, "k")
            evac(i - 3, "hg")
            store(i - 3, "hg")
            t1c(i - 1)
            scale_k(i - 3)
            regroup(i - 2)
            scale_q(i - 3)
            quantise(i - 2)
            gate(i)
